import numpy as np
import ml_dtypes


def mxq(x, axis, fmt="e4m3"):
    dtype, down = {"e4m3": (ml_dtypes.float8_e4m3fn, 7), "e5m2": (ml_dtypes.float8_e5m2, 14)}[fmt]
    v = np.moveaxis(np.asarray(x, np.float32).astype(ml_dtypes.bfloat16).astype(np.float64), axis, -1)
    blocks = v.reshape(v.shape[:-1] + (-1, 32))
    amax = np.abs(blocks).max(-1, keepdims=True)
    byte = np.maximum(np.where(amax > 0, np.frexp(amax)[1] - 1 + 127, 0) - down, 1)
    scale = np.exp2(byte - 127.0)
    codes = (blocks / scale).astype(np.float32).astype(dtype).astype(np.float64)
    return np.moveaxis((codes * scale).reshape(v.shape), -1, axis)


WIDE = False


def mx_kscale(k):
    if not WIDE:
        return np.ones(k)
    levels = np.array([10, -10, 5, -5, 0])
    if k % 512:
        return np.exp2(np.random.permutation(np.resize(levels, k // 32))).repeat(32)
    a = np.empty((k // 512, 16))
    for p in range(k // 512):
        a[p, :8] = np.random.permutation(np.resize(levels, 8))
        for g in range(8):
            far = levels[np.abs(levels - a[p, g]) >= 10]
            a[p, g + 8] = far[np.random.randint(len(far))]
    return np.exp2(a.ravel()).repeat(32)


BF16 = ml_dtypes.bfloat16


def bf(x):
    return np.asarray(x, np.float32).astype(BF16)


def f64(x):
    return np.asarray(x).astype(np.float64)


B, S, HID, NH, HD, RD, RATIO = 1, 2048, 1024, 8, 128, 64, 4
THETA = 10000.0
HALF = RD // 2


def rope_tables(positions):
    inv_freq = 1.0 / THETA ** (np.arange(HALF) / HALF)
    ang = positions[:, None] * inv_freq[None, :]
    return np.cos(ang), np.sin(ang)


def rope_interleaved(x, cos, sin):
    nope, rope = x[..., :-RD], x[..., -RD:]
    pr = rope.reshape(rope.shape[:-1] + (HALF, 2))
    a, b = pr[..., 0], pr[..., 1]
    new = np.stack([a * cos - b * sin, a * sin + b * cos], axis=-1).reshape(rope.shape)
    return np.concatenate([nope, new], axis=-1)


def setup_inputs():
    s = mx_kscale(HID)
    return {"hidden": bf(np.random.standard_normal((B, S, HID)) * s),
            "wq": bf(np.random.standard_normal((HID, NH * HD)) / np.sqrt(HID) / s[:, None])}


def reference(hidden, wq):
    q = mxq(f64(hidden), 2, "e4m3") @ mxq(f64(wq), 0, "e4m3")
    q = q.reshape(B, S, NH, HD).transpose(0, 2, 1, 3)
    cq, sq = rope_tables(np.arange(S))
    return rope_interleaved(q, cq, sq)

@@ -1,0 +1,245 @@
+import math
+from contextlib import ExitStack
+
+import concourse.mybir as mybir
+from concourse.masks import make_identity
+
+F32 = mybir.dt.float32
+BF16 = mybir.dt.bfloat16
+I32 = mybir.dt.int32
+U32 = mybir.dt.uint32
+U8 = mybir.dt.uint8
+FP8X4 = mybir.dt.float8_e4m3fn_x4
+ALU = mybir.AluOpType
+ACT = mybir.ActivationFunctionType
+
+P = 128
+TOKENS = 2048
+HIDDEN = 1024
+HEADS = 8
+HEAD_DIM = 128
+PAIRS = 32
+PLAIN = HEAD_DIM - 2 * PAIRS
+THETA = 10000.0
+
+PACK = 4
+HALVES = 2
+K_PASS = P * PACK
+PASSES = HIDDEN // K_PASS
+BANK = 512
+
+TILES = TOKENS // P
+GROUP = 2
+GROUPS = TILES // GROUP
+AHEAD = 2
+
+ROTATED = 0
+COPIED = 1
+
+FLOPS = 2 * TOKENS * HIDDEN * HEADS * HEAD_DIM
+
+
+def tile_deepseekv4attention_pb_kernel(tc, hidden, wq, out):
+    nc = tc.nc
+    with ExitStack() as ctx:
+        keep = ctx.enter_context(tc.tile_pool(name="keep", bufs=1))
+        w_stage = ctx.enter_context(tc.tile_pool(name="w_stage", bufs=2))
+        h_stage = ctx.enter_context(tc.tile_pool(name="h_stage", bufs=AHEAD + 2))
+        work = ctx.enter_context(tc.tile_pool(name="work", bufs=3))
+        flipped_banks = ctx.enter_context(tc.psum_pool(name="flipped_banks", bufs=GROUP))
+        rotated_banks = ctx.enter_context(tc.psum_pool(name="rotated_banks", bufs=3))
+        copied_banks = ctx.enter_context(tc.psum_pool(name="copied_banks", bufs=3))
+        ctx.enter_context(tc.manual_schedule())
+
+        hidden_groups = hidden[0].rearrange("(p n x) k -> n p (x k)", n=GROUPS, x=GROUP)
+        out_groups = out[0].rearrange("h (p n x) d -> n p h (x d)", n=GROUPS, x=GROUP)
+        out_tiles = out[0].rearrange("h (p i) d -> i p h d", i=TILES)
+
+        h_raw = []
+        for n in range(GROUPS):
+            h_raw.append(keep.tile([P, GROUP * HIDDEN], BF16, name="h_raw%d" % n))
+        w_raw = keep.tile([P, PASSES, PACK, HEADS * HEAD_DIM], BF16)
+
+        def load_wq(g):
+            nc.sync.dma_start(
+                out=w_raw[:, g].rearrange("q t n -> q (t n)"),
+                in_=wq[g * K_PASS : (g + 1) * K_PASS, :].rearrange("(q t) n -> q (t n)", q=P),
+            )
+
+        for g in range(PASSES):
+            load_wq(g)
+        for n in range(GROUPS):
+            nc.sync.dma_start(out=h_raw[n][:], in_=hidden_groups[n])
+
+        table = keep.tile([P, TILES, 2, 2, PAIRS], F32)
+
+        warm = keep.tile([P, 1], F32)
+        nc.vector.memset(warm[:], 0.0)
+        nc.scalar.activation(out=warm[:], in_=warm[:], func=ACT.Sin)
+
+        token_int = keep.tile([P, TILES], I32)
+        nc.gpsimd.iota(token_int[:], pattern=[[1, TILES]], base=0, channel_multiplier=TILES)
+        identity = keep.tile([P, P], F32)
+        make_identity(nc, identity[:])
+        token = keep.tile([P, TILES], F32)
+        nc.vector.tensor_copy(out=token[:], in_=token_int[:])
+
+        turns = keep.tile([P, TILES, PAIRS], F32)
+        for j in range(PAIRS):
+            nc.vector.tensor_scalar(
+                out=turns[:, :, j],
+                in0=token[:],
+                scalar1=THETA ** (-j / PAIRS) / (2.0 * math.pi),
+                scalar2=None,
+                op0=ALU.mult,
+            )
+        whole = keep.tile([P, TILES, PAIRS], I32)
+        nc.vector.tensor_copy(out=whole[:], in_=turns[:])
+        fraction = keep.tile([P, TILES, PAIRS], F32)
+        nc.vector.tensor_tensor(out=fraction[:], in0=turns[:], in1=whole[:], op=ALU.subtract)
+        minus_abs = keep.tile([P, TILES, PAIRS], F32)
+        nc.vector.scalar_tensor_tensor(
+            out=minus_abs[:], in0=fraction[:], scalar=-1.0, in1=fraction[:], op0=ALU.mult, op1=ALU.min
+        )
+        quarter_less_abs = keep.tile([P, TILES, PAIRS], F32)
+        nc.vector.tensor_scalar(
+            out=quarter_less_abs[:], in0=minus_abs[:], scalar1=0.25, scalar2=None, op0=ALU.add
+        )
+        turn = 2.0 * math.pi
+        nc.scalar.activation(out=table[:, :, 0, 1, :], in_=fraction[:], func=ACT.Sin, scale=-turn)
+        nc.scalar.activation(out=table[:, :, 1, 0, :], in_=fraction[:], func=ACT.Sin, scale=turn)
+        for s in range(2):
+            nc.scalar.activation(
+                out=table[:, :, s, s, :], in_=quarter_less_abs[:], func=ACT.Sin, scale=turn
+            )
+
+        def transpose_hidden(n):
+            raw_words = h_raw[n][:].bitcast(F32).rearrange("m (x w) -> m x w", x=GROUP)
+            grouped = h_stage.tile([P, GROUP * PASSES * P * PACK], BF16, align_bytes=64)
+            grouped_words = grouped[:].bitcast(F32).rearrange(
+                "q (x g m u) -> q x g m u", x=GROUP, g=PASSES, u=HALVES
+            )
+            for x in range(GROUP):
+                flipped = flipped_banks.tile([P, PASSES * HALVES, P], F32)
+                for g in range(PASSES):
+                    for u in range(HALVES):
+                        nc.tensor.transpose(
+                            flipped[:, g * HALVES + u, :],
+                            raw_words[:, x, g * HALVES * P + u : (g + 1) * HALVES * P : HALVES],
+                            identity[:],
+                        )
+                nc.scalar.copy(
+                    out=grouped_words[:, x],
+                    in_=flipped[:].rearrange("q (g u) m -> q g m u", u=HALVES),
+                )
+            return grouped
+
+        def quantise_hidden(grouped):
+            codes = h_stage.tile([P, GROUP * PASSES * P], U32, align_bytes=64)
+            scales = h_stage.tile([P, GROUP * PASSES * P], U8, align_bytes=64)
+            nc.vector.quantize_mx(out=codes[:].bitcast(FP8X4), scales=scales[:], in_=grouped[:])
+            return codes, scales
+
+        w_codes = keep.tile([P, PASSES, 2, BANK], U32, align_bytes=64)
+        w_scales = keep.tile([P, PASSES, 2, BANK], U8, align_bytes=64)
+
+        def features_of_wq(g):
+            return w_raw[:, g].rearrange("q t (h s c) -> q s h c t", h=HEADS, s=2)
+
+        def regroup_rotated(g):
+            grouped = w_stage.tile([P, BANK * PACK], BF16, align_bytes=64, tag="rotated")
+            pairs_out = grouped[:].rearrange("q (r h j t) -> q r h j t", r=2, h=HEADS, t=PACK)
+            pairs_in = features_of_wq(g)[:, 1].rearrange("q h (j r) t -> q r h j t", r=2)
+            for r in range(2):
+                nc.vector.tensor_copy(out=pairs_out[:, r], in_=pairs_in[:, r])
+            return grouped
+
+        def regroup_copied(g, copy):
+            grouped = w_stage.tile([P, BANK * PACK], BF16, align_bytes=64, tag="copied")
+            copy(
+                out=grouped[:].rearrange("q (h c t) -> q h c t", h=HEADS, t=PACK),
+                in_=features_of_wq(g)[:, 0],
+            )
+            return grouped
+
+        def quantise_wq(g, part, grouped):
+            nc.vector.quantize_mx(
+                out=w_codes[:, g, part, :].bitcast(FP8X4),
+                scales=w_scales[:, g, part, :],
+                in_=grouped[:],
+            )
+
+        def project(n, codes, scales):
+            result = work.tile([P, HEADS, GROUP, HEAD_DIM], F32)
+            products = work.tile([P, 2, 2, HEADS, GROUP, PAIRS], F32)
+            for x in range(GROUP):
+                rotated_acc = rotated_banks.tile([P, BANK], F32)
+                copied_acc = copied_banks.tile([P, BANK], F32)
+                for part, acc in ((ROTATED, rotated_acc), (COPIED, copied_acc)):
+                    for g in range(PASSES):
+                        tokens = slice((x * PASSES + g) * P, (x * PASSES + g + 1) * P)
+                        nc.tensor.matmul_mx(
+                            out=acc[:],
+                            lhsT=codes[:, tokens].bitcast(FP8X4),
+                            lhsT_scale=scales[:, tokens],
+                            rhs=w_codes[:, g, part, :].bitcast(FP8X4),
+                            rhs_scale=w_scales[:, g, part, :],
+                            start=(g == 0),
+                            stop=(g == PASSES - 1),
+                        )
+                shape = [P, 2, 2, HEADS, PAIRS]
+                nc.vector.tensor_tensor(
+                    out=products[:, :, :, :, x, :],
+                    in0=rotated_acc[:]
+                    .rearrange("p (r h j) -> p r h j", r=2, h=HEADS)
+                    .unsqueeze(1)
+                    .to_broadcast(shape),
+                    in1=table[:, n * GROUP + x].unsqueeze(3).to_broadcast(shape),
+                    op=ALU.mult,
+                )
+                nc.scalar.copy(
+                    out=result[:, :, x, :PLAIN],
+                    in_=copied_acc[:].rearrange("p (h c) -> p h c", h=HEADS),
+                )
+            return result, products
+
+        def sum_and_store(n, result, products):
+            if n < GROUPS - 1:
+                nc.gpsimd.tensor_tensor(
+                    out=result[:, :, :, PLAIN:].rearrange("p h x (j s) -> p h x j s", s=2),
+                    in0=products[:, :, 0].rearrange("p s h x j -> p h x j s"),
+                    in1=products[:, :, 1].rearrange("p s h x j -> p h x j s"),
+                    op=ALU.add,
+                )
+                nc.sync.dma_start(
+                    out=out_groups[n], in_=result[:].rearrange("p h x d -> p h (x d)")
+                )
+            else:
+                for x in range(GROUP):
+                    nc.vector.tensor_tensor(
+                        out=result[:, :, x, PLAIN:].rearrange("p h (j s) -> p h j s", s=2),
+                        in0=products[:, :, 0, :, x, :].rearrange("p s h j -> p h j s"),
+                        in1=products[:, :, 1, :, x, :].rearrange("p s h j -> p h j s"),
+                        op=ALU.add,
+                    )
+                    nc.sync.dma_start(out=out_tiles[n * GROUP + x], in_=result[:, :, x, :])
+
+        rotated_0 = regroup_rotated(0)
+        copied_0 = regroup_copied(0, nc.scalar.copy)
+        quantise_wq(0, ROTATED, rotated_0)
+        rotated_1 = regroup_rotated(1)
+        quantise_wq(1, ROTATED, rotated_1)
+        copied_1 = regroup_copied(1, nc.vector.tensor_copy)
+        quantise_wq(0, COPIED, copied_0)
+        quantise_wq(1, COPIED, copied_1)
+        quantised = {}
+        for n in range(AHEAD):
+            quantised[n] = quantise_hidden(transpose_hidden(n))
+
+        for n in range(GROUPS):
+            if n + AHEAD < GROUPS:
+                grouped = transpose_hidden(n + AHEAD)
+            result, products = project(n, quantised[n][0], quantised[n][1])
+            if n + AHEAD < GROUPS:
+                quantised[n + AHEAD] = quantise_hidden(grouped)
+            sum_and_store(n, result, products)

@@ -204,25 +204,20 @@ def tile_deepseekv4attention_pb_kernel(tc, hidden, wq, out):
             return result, products
 
         def sum_and_store(n, result, products):
-            if n < GROUPS - 1:
-                nc.gpsimd.tensor_tensor(
-                    out=result[:, :, :, PLAIN:].rearrange("p h x (j s) -> p h x j s", s=2),
-                    in0=products[:, :, 0].rearrange("p s h x j -> p h x j s"),
-                    in1=products[:, :, 1].rearrange("p s h x j -> p h x j s"),
+            for x in range(GROUP):
+                adder = nc.vector if n * GROUP + x == TILES - 1 else nc.gpsimd
+                adder.tensor_tensor(
+                    out=result[:, :, x, PLAIN:].rearrange("p h (j s) -> p h j s", s=2),
+                    in0=products[:, :, 0, :, x, :].rearrange("p s h j -> p h j s"),
+                    in1=products[:, :, 1, :, x, :].rearrange("p s h j -> p h j s"),
                     op=ALU.add,
                 )
+                if n >= GROUPS - 2:
+                    nc.sync.dma_start(out=out_tiles[n * GROUP + x], in_=result[:, :, x, :])
+            if n < GROUPS - 2:
                 nc.sync.dma_start(
                     out=out_groups[n], in_=result[:].rearrange("p h x d -> p h (x d)")
                 )
-            else:
-                for x in range(GROUP):
-                    nc.vector.tensor_tensor(
-                        out=result[:, :, x, PLAIN:].rearrange("p h (j s) -> p h j s", s=2),
-                        in0=products[:, :, 0, :, x, :].rearrange("p s h j -> p h j s"),
-                        in1=products[:, :, 1, :, x, :].rearrange("p s h j -> p h j s"),
-                        op=ALU.add,
-                    )
-                    nc.sync.dma_start(out=out_tiles[n * GROUP + x], in_=result[:, :, x, :])
 
         rotated_0 = regroup_rotated(0)
         copied_0 = regroup_copied(0, nc.scalar.copy)

@@ -85,14 +85,21 @@ def tile_deepseekv4attention_pb_kernel(tc, hidden, wq, out):
         nc.vector.tensor_copy(out=token[:], in_=token_int[:])
 
         turns = keep.tile([P, TILES, PAIRS], F32)
-        for j in range(PAIRS):
+        ratio = THETA ** (-1.0 / PAIRS)
+        for j in range(4):
             nc.vector.tensor_scalar(
-                out=turns[:, :, j],
-                in0=token[:],
-                scalar1=THETA ** (-j / PAIRS) / (2.0 * math.pi),
-                scalar2=None,
+                out=turns[:, :, j], in0=token[:], scalar1=ratio**j / (2.0 * math.pi), scalar2=None,
                 op0=ALU.mult,
             )
+        for first in (4, 8, 12):
+            nc.vector.tensor_scalar(
+                out=turns[:, :, first : first + 4], in0=turns[:, :, 0:4], scalar1=ratio**first,
+                scalar2=None, op0=ALU.mult,
+            )
+        nc.vector.tensor_scalar(
+            out=turns[:, :, 16:32], in0=turns[:, :, 0:16], scalar1=ratio**16, scalar2=None,
+            op0=ALU.mult,
+        )
         whole = keep.tile([P, TILES, PAIRS], I32)
         nc.vector.tensor_copy(out=whole[:], in_=turns[:])
         fraction = keep.tile([P, TILES, PAIRS], F32)
@@ -101,16 +108,13 @@ def tile_deepseekv4attention_pb_kernel(tc, hidden, wq, out):
         nc.vector.scalar_tensor_tensor(
             out=minus_abs[:], in0=fraction[:], scalar=-1.0, in1=fraction[:], op0=ALU.mult, op1=ALU.min
         )
-        quarter_less_abs = keep.tile([P, TILES, PAIRS], F32)
-        nc.vector.tensor_scalar(
-            out=quarter_less_abs[:], in0=minus_abs[:], scalar1=0.25, scalar2=None, op0=ALU.add
-        )
         turn = 2.0 * math.pi
         nc.scalar.activation(out=table[:, :, 0, 1, :], in_=fraction[:], func=ACT.Sin, scale=-turn)
         nc.scalar.activation(out=table[:, :, 1, 0, :], in_=fraction[:], func=ACT.Sin, scale=turn)
         for s in range(2):
             nc.scalar.activation(
-                out=table[:, :, s, s, :], in_=quarter_less_abs[:], func=ACT.Sin, scale=turn
+                out=table[:, :, s, s, :], in_=minus_abs[:], func=ACT.Sin, scale=turn,
+                bias=0.5 * math.pi,
             )
 
         def transpose_hidden(n):

@@ -223,6 +223,13 @@ def tile_deepseekv4attention_pb_kernel(tc, hidden, wq, out):
                     out=out_groups[n], in_=result[:].rearrange("p h x d -> p h (x d)")
                 )
 
+        def keep_clock_up(fresh, count):
+            unused = copied_banks.tile([P, BANK], F32, name="copied_acc")
+            for c in range(count):
+                nc.tensor.matmul(
+                    unused[:], lhsT=fresh[:, :P], rhs=fresh[:, :BANK], start=True, stop=True
+                )
+
         rotated_0 = regroup_rotated(0)
         copied_0 = regroup_copied(0, nc.scalar.copy)
         quantise_wq(0, ROTATED, rotated_0)
@@ -232,8 +239,11 @@ def tile_deepseekv4attention_pb_kernel(tc, hidden, wq, out):
         quantise_wq(0, COPIED, copied_0)
         quantise_wq(1, COPIED, copied_1)
         quantised = {}
+        for g in range(PASSES):
+            keep_clock_up(w_raw[:, g, 0, :], 3)
         for n in range(AHEAD):
             quantised[n] = quantise_hidden(transpose_hidden(n))
+        keep_clock_up(h_raw[AHEAD - 1][:], 2)
 
         for n in range(GROUPS):
             if n + AHEAD < GROUPS:

@@ -31,6 +31,8 @@ BANK = 512
 TILES = TOKENS // P
 GROUP = 2
 GROUPS = TILES // GROUP
+GPSIMD_HEADS = slice(0, 4)
+VECTOR_HEADS = slice(4, 8)
 AHEAD = 2
 
 ROTATED = 0
@@ -173,55 +175,52 @@ def tile_deepseekv4attention_pb_kernel(tc, hidden, wq, out):
                 in_=grouped[:],
             )
 
-        def project(n, codes, scales):
-            result = work.tile([P, HEADS, GROUP, HEAD_DIM], F32)
-            products = work.tile([P, 2, 2, HEADS, GROUP, PAIRS], F32)
-            for x in range(GROUP):
-                rotated_acc = rotated_banks.tile([P, BANK], F32)
-                copied_acc = copied_banks.tile([P, BANK], F32)
-                for part, acc in ((ROTATED, rotated_acc), (COPIED, copied_acc)):
-                    for g in range(PASSES):
-                        tokens = slice((x * PASSES + g) * P, (x * PASSES + g + 1) * P)
-                        nc.tensor.matmul_mx(
-                            out=acc[:],
-                            lhsT=codes[:, tokens].bitcast(FP8X4),
-                            lhsT_scale=scales[:, tokens],
-                            rhs=w_codes[:, g, part, :].bitcast(FP8X4),
-                            rhs_scale=w_scales[:, g, part, :],
-                            start=(g == 0),
-                            stop=(g == PASSES - 1),
-                        )
-                shape = [P, 2, 2, HEADS, PAIRS]
-                nc.vector.tensor_tensor(
-                    out=products[:, :, :, :, x, :],
-                    in0=rotated_acc[:]
-                    .rearrange("p (r h j) -> p r h j", r=2, h=HEADS)
-                    .unsqueeze(1)
-                    .to_broadcast(shape),
-                    in1=table[:, n * GROUP + x].unsqueeze(3).to_broadcast(shape),
-                    op=ALU.mult,
-                )
-                nc.scalar.copy(
-                    out=result[:, :, x, :PLAIN],
-                    in_=copied_acc[:].rearrange("p (h c) -> p h c", h=HEADS),
-                )
-            return result, products
+        def project(n, x, result, products):
+            codes, scales = quantised[n]
+            rotated_acc = rotated_banks.tile([P, BANK], F32)
+            copied_acc = copied_banks.tile([P, BANK], F32)
+            for part, acc in ((ROTATED, rotated_acc), (COPIED, copied_acc)):
+                for g in range(PASSES):
+                    tokens = slice((x * PASSES + g) * P, (x * PASSES + g + 1) * P)
+                    nc.tensor.matmul_mx(
+                        out=acc[:],
+                        lhsT=codes[:, tokens].bitcast(FP8X4),
+                        lhsT_scale=scales[:, tokens],
+                        rhs=w_codes[:, g, part, :].bitcast(FP8X4),
+                        rhs_scale=w_scales[:, g, part, :],
+                        start=(g == 0),
+                        stop=(g == PASSES - 1),
+                    )
+            shape = [P, 2, 2, HEADS, PAIRS]
+            nc.vector.tensor_tensor(
+                out=products[:, :, :, :, x, :],
+                in0=rotated_acc[:]
+                .rearrange("p (r h j) -> p r h j", r=2, h=HEADS)
+                .unsqueeze(1)
+                .to_broadcast(shape),
+                in1=table[:, n * GROUP + x].unsqueeze(3).to_broadcast(shape),
+                op=ALU.mult,
+            )
+            nc.scalar.copy(
+                out=result[:, :, x, :PLAIN],
+                in_=copied_acc[:].rearrange("p (h c) -> p h c", h=HEADS),
+            )
 
-        def sum_and_store(n, result, products):
-            for x in range(GROUP):
-                adder = nc.vector if n * GROUP + x == TILES - 1 else nc.gpsimd
-                adder.tensor_tensor(
-                    out=result[:, :, x, PLAIN:].rearrange("p h (j s) -> p h j s", s=2),
-                    in0=products[:, :, 0, :, x, :].rearrange("p s h j -> p h j s"),
-                    in1=products[:, :, 1, :, x, :].rearrange("p s h j -> p h j s"),
-                    op=ALU.add,
-                )
-                if n >= GROUPS - 2:
-                    nc.sync.dma_start(out=out_tiles[n * GROUP + x], in_=result[:, :, x, :])
-            if n < GROUPS - 2:
-                nc.sync.dma_start(
-                    out=out_groups[n], in_=result[:].rearrange("p h x d -> p h (x d)")
-                )
+        def add_tile(engine, heads, x, result, products):
+            engine.tensor_tensor(
+                out=result[:, heads, x, PLAIN:].rearrange("p h (j s) -> p h j s", s=2),
+                in0=products[:, :, 0, heads, x, :].rearrange("p s h j -> p h j s"),
+                in1=products[:, :, 1, heads, x, :].rearrange("p s h j -> p h j s"),
+                op=ALU.add,
+            )
+
+        def add_group(engine, heads, result, products):
+            engine.tensor_tensor(
+                out=result[:, heads, :, PLAIN:].rearrange("p h x (j s) -> p h x j s", s=2),
+                in0=products[:, :, 0, heads].rearrange("p s h x j -> p h x j s"),
+                in1=products[:, :, 1, heads].rearrange("p s h x j -> p h x j s"),
+                op=ALU.add,
+            )
 
         def keep_clock_up(fresh, count):
             unused = copied_banks.tile([P, BANK], F32, name="copied_acc")
@@ -248,7 +247,29 @@ def tile_deepseekv4attention_pb_kernel(tc, hidden, wq, out):
         for n in range(GROUPS):
             if n + AHEAD < GROUPS:
                 grouped = transpose_hidden(n + AHEAD)
-            result, products = project(n, quantised[n][0], quantised[n][1])
-            if n + AHEAD < GROUPS:
+            result = work.tile([P, HEADS, GROUP, HEAD_DIM], F32)
+            products = work.tile([P, 2, 2, HEADS, GROUP, PAIRS], F32)
+            by_tile = n >= GROUPS - 2
+            project(n, 0, result, products)
+            if by_tile:
+                add_tile(nc.vector, VECTOR_HEADS, 0, result, products)
+            else:
                 quantised[n + AHEAD] = quantise_hidden(grouped)
-            sum_and_store(n, result, products)
+            add_tile(nc.gpsimd, GPSIMD_HEADS, 0, result, products)
+            if by_tile:
+                nc.sync.dma_start(out=out_tiles[n * GROUP], in_=result[:, :, 0, :])
+            project(n, 1, result, products)
+            if n == GROUPS - 1:
+                add_tile(nc.vector, slice(0, HEADS), 1, result, products)
+            elif by_tile:
+                add_tile(nc.vector, VECTOR_HEADS, 1, result, products)
+                add_tile(nc.gpsimd, GPSIMD_HEADS, 1, result, products)
+            else:
+                add_group(nc.vector, VECTOR_HEADS, result, products)
+                add_tile(nc.gpsimd, GPSIMD_HEADS, 1, result, products)
+            if by_tile:
+                nc.sync.dma_start(out=out_tiles[n * GROUP + 1], in_=result[:, :, 1, :])
+            else:
+                nc.sync.dma_start(
+                    out=out_groups[n], in_=result[:].rearrange("p h x d -> p h (x d)")
+                )

@@ -47,7 +47,7 @@ def tile_deepseekv4attention_pb_kernel(tc, hidden, wq, out):
         keep = ctx.enter_context(tc.tile_pool(name="keep", bufs=1))
         w_stage = ctx.enter_context(tc.tile_pool(name="w_stage", bufs=2))
         h_stage = ctx.enter_context(tc.tile_pool(name="h_stage", bufs=AHEAD + 2))
-        work = ctx.enter_context(tc.tile_pool(name="work", bufs=3))
+        work = ctx.enter_context(tc.tile_pool(name="work", bufs=4))
         flipped_banks = ctx.enter_context(tc.psum_pool(name="flipped_banks", bufs=GROUP))
         rotated_banks = ctx.enter_context(tc.psum_pool(name="rotated_banks", bufs=3))
         copied_banks = ctx.enter_context(tc.psum_pool(name="copied_banks", bufs=3))
@@ -244,6 +244,7 @@ def tile_deepseekv4attention_pb_kernel(tc, hidden, wq, out):
             quantised[n] = quantise_hidden(transpose_hidden(n))
         keep_clock_up(h_raw[AHEAD - 1][:], 2)
 
+        earlier = None
         for n in range(GROUPS):
             if n + AHEAD < GROUPS:
                 grouped = transpose_hidden(n + AHEAD)
@@ -251,25 +252,23 @@ def tile_deepseekv4attention_pb_kernel(tc, hidden, wq, out):
             products = work.tile([P, 2, 2, HEADS, GROUP, PAIRS], F32)
             by_tile = n >= GROUPS - 2
             project(n, 0, result, products)
+            if n == GROUPS - 1:
+                add_tile(nc.vector, VECTOR_HEADS, 1, earlier[0], earlier[1])
+                nc.sync.dma_start(out=out_tiles[n * GROUP - 1], in_=earlier[0][:, :, 1, :])
+            elif n > 0:
+                add_group(nc.vector, VECTOR_HEADS, earlier[0], earlier[1])
+                nc.sync.dma_start(
+                    out=out_groups[n - 1], in_=earlier[0][:].rearrange("p h x d -> p h (x d)")
+                )
+            add_tile(nc.gpsimd, GPSIMD_HEADS, 0, result, products)
+            project(n, 1, result, products)
             if by_tile:
                 add_tile(nc.vector, VECTOR_HEADS, 0, result, products)
+                nc.sync.dma_start(out=out_tiles[n * GROUP], in_=result[:, :, 0, :])
             else:
                 quantised[n + AHEAD] = quantise_hidden(grouped)
-            add_tile(nc.gpsimd, GPSIMD_HEADS, 0, result, products)
-            if by_tile:
-                nc.sync.dma_start(out=out_tiles[n * GROUP], in_=result[:, :, 0, :])
-            project(n, 1, result, products)
-            if n == GROUPS - 1:
-                add_tile(nc.vector, slice(0, HEADS), 1, result, products)
-            elif by_tile:
-                add_tile(nc.vector, VECTOR_HEADS, 1, result, products)
+            if n < GROUPS - 1:
                 add_tile(nc.gpsimd, GPSIMD_HEADS, 1, result, products)
-            else:
-                add_group(nc.vector, VECTOR_HEADS, result, products)
-                add_tile(nc.gpsimd, GPSIMD_HEADS, 1, result, products)
-            if by_tile:
-                nc.sync.dma_start(out=out_tiles[n * GROUP + 1], in_=result[:, :, 1, :])
-            else:
-                nc.sync.dma_start(
-                    out=out_groups[n], in_=result[:].rearrange("p h x d -> p h (x d)")
-                )
+            earlier = (result, products)
+        add_tile(nc.vector, slice(0, HEADS), 1, earlier[0], earlier[1])
+        nc.sync.dma_start(out=out_tiles[TILES - 1], in_=earlier[0][:, :, 1, :])

@@ -48,9 +48,9 @@ def tile_deepseekv4attention_pb_kernel(tc, hidden, wq, out):
         w_stage = ctx.enter_context(tc.tile_pool(name="w_stage", bufs=2))
         h_stage = ctx.enter_context(tc.tile_pool(name="h_stage", bufs=AHEAD + 2))
         work = ctx.enter_context(tc.tile_pool(name="work", bufs=4))
-        flipped_banks = ctx.enter_context(tc.psum_pool(name="flipped_banks", bufs=GROUP))
+        flipped_banks = ctx.enter_context(tc.psum_pool(name="flipped_banks", bufs=3))
         rotated_banks = ctx.enter_context(tc.psum_pool(name="rotated_banks", bufs=3))
-        copied_banks = ctx.enter_context(tc.psum_pool(name="copied_banks", bufs=3))
+        copied_banks = ctx.enter_context(tc.psum_pool(name="copied_banks", bufs=2))
         ctx.enter_context(tc.manual_schedule())
 
         hidden_groups = hidden[0].rearrange("(p n x) k -> n p (x k)", n=GROUPS, x=GROUP)

@@ -31,8 +31,8 @@ BANK = 512
 TILES = TOKENS // P
 GROUP = 2
 GROUPS = TILES // GROUP
-GPSIMD_HEADS = slice(0, 4)
-VECTOR_HEADS = slice(4, 8)
+GPSIMD_HEADS = slice(0, 6)
+VECTOR_HEADS = slice(6, 8)
 AHEAD = 2
 
 ROTATED = 0

@@ -154,10 +154,10 @@ def tile_deepseekv4attention_pb_kernel(tc, hidden, wq, out):
 
         def regroup_rotated(g):
             grouped = w_stage.tile([P, BANK * PACK], BF16, align_bytes=64, tag="rotated")
-            pairs_out = grouped[:].rearrange("q (r h j t) -> q r h j t", r=2, h=HEADS, t=PACK)
-            pairs_in = features_of_wq(g)[:, 1].rearrange("q h (j r) t -> q r h j t", r=2)
-            for r in range(2):
-                nc.vector.tensor_copy(out=pairs_out[:, r], in_=pairs_in[:, r])
+            nc.vector.tensor_copy(
+                out=grouped[:].rearrange("q (h r j t) -> q h r j t", r=2, h=HEADS, t=PACK),
+                in_=features_of_wq(g)[:, 1].rearrange("q h (j r) t -> q h r j t", r=2),
+            )
             return grouped
 
         def regroup_copied(g, copy):
@@ -191,14 +191,17 @@ def tile_deepseekv4attention_pb_kernel(tc, hidden, wq, out):
                         start=(g == 0),
                         stop=(g == PASSES - 1),
                     )
-            shape = [P, 2, 2, HEADS, PAIRS]
+            shape = [P, HEADS, 2, PAIRS, 2]
             nc.vector.tensor_tensor(
-                out=products[:, :, :, :, x, :],
+                out=products[:, :, :, x].rearrange("p r h j s -> p h r j s"),
                 in0=rotated_acc[:]
-                .rearrange("p (r h j) -> p r h j", r=2, h=HEADS)
+                .rearrange("p (h r j) -> p h r j", r=2, h=HEADS)
+                .unsqueeze(4)
+                .to_broadcast(shape),
+                in1=table[:, n * GROUP + x]
+                .rearrange("p s r j -> p r j s")
                 .unsqueeze(1)
                 .to_broadcast(shape),
-                in1=table[:, n * GROUP + x].unsqueeze(3).to_broadcast(shape),
                 op=ALU.mult,
             )
             nc.scalar.copy(
@@ -208,17 +211,17 @@ def tile_deepseekv4attention_pb_kernel(tc, hidden, wq, out):
 
         def add_tile(engine, heads, x, result, products):
             engine.tensor_tensor(
-                out=result[:, heads, x, PLAIN:].rearrange("p h (j s) -> p h j s", s=2),
-                in0=products[:, :, 0, heads, x, :].rearrange("p s h j -> p h j s"),
-                in1=products[:, :, 1, heads, x, :].rearrange("p s h j -> p h j s"),
+                out=result[:, heads, x, PLAIN:],
+                in0=products[:, 0, heads, x].rearrange("p h j s -> p h (j s)"),
+                in1=products[:, 1, heads, x].rearrange("p h j s -> p h (j s)"),
                 op=ALU.add,
             )
 
         def add_group(engine, heads, result, products):
             engine.tensor_tensor(
-                out=result[:, heads, :, PLAIN:].rearrange("p h x (j s) -> p h x j s", s=2),
-                in0=products[:, :, 0, heads].rearrange("p s h x j -> p h x j s"),
-                in1=products[:, :, 1, heads].rearrange("p s h x j -> p h x j s"),
+                out=result[:, heads, :, PLAIN:],
+                in0=products[:, 0, heads].rearrange("p h x j s -> p h x (j s)"),
+                in1=products[:, 1, heads].rearrange("p h x j s -> p h x (j s)"),
                 op=ALU.add,
             )
 
@@ -249,7 +252,7 @@ def tile_deepseekv4attention_pb_kernel(tc, hidden, wq, out):
             if n + AHEAD < GROUPS:
                 grouped = transpose_hidden(n + AHEAD)
             result = work.tile([P, HEADS, GROUP, HEAD_DIM], F32)
-            products = work.tile([P, 2, 2, HEADS, GROUP, PAIRS], F32)
+            products = work.tile([P, 2, HEADS, GROUP, PAIRS, 2], F32)
             by_tile = n >= GROUPS - 2
             project(n, 0, result, products)
             if n == GROUPS - 1:

@@ -175,22 +175,34 @@ def tile_deepseekv4attention_pb_kernel(tc, hidden, wq, out):
                 in_=grouped[:],
             )
 
-        def project(n, x, result, products):
+        def multiply(n, x, part, acc):
             codes, scales = quantised[n]
+            for g in range(PASSES):
+                tokens = slice((x * PASSES + g) * P, (x * PASSES + g + 1) * P)
+                nc.tensor.matmul_mx(
+                    out=acc[:],
+                    lhsT=codes[:, tokens].bitcast(FP8X4),
+                    lhsT_scale=scales[:, tokens],
+                    rhs=w_codes[:, g, part, :].bitcast(FP8X4),
+                    rhs_scale=w_scales[:, g, part, :],
+                    start=(g == 0),
+                    stop=(g == PASSES - 1),
+                )
+
+        def multiply_rotated(n, x):
             rotated_acc = rotated_banks.tile([P, BANK], F32)
+            multiply(n, x, ROTATED, rotated_acc)
+            return rotated_acc
+
+        def multiply_copied(n, x, result):
             copied_acc = copied_banks.tile([P, BANK], F32)
-            for part, acc in ((ROTATED, rotated_acc), (COPIED, copied_acc)):
-                for g in range(PASSES):
-                    tokens = slice((x * PASSES + g) * P, (x * PASSES + g + 1) * P)
-                    nc.tensor.matmul_mx(
-                        out=acc[:],
-                        lhsT=codes[:, tokens].bitcast(FP8X4),
-                        lhsT_scale=scales[:, tokens],
-                        rhs=w_codes[:, g, part, :].bitcast(FP8X4),
-                        rhs_scale=w_scales[:, g, part, :],
-                        start=(g == 0),
-                        stop=(g == PASSES - 1),
-                    )
+            multiply(n, x, COPIED, copied_acc)
+            nc.scalar.copy(
+                out=result[:, :, x, :PLAIN],
+                in_=copied_acc[:].rearrange("p (h c) -> p h c", h=HEADS),
+            )
+
+        def rotate(n, x, rotated_acc, products):
             shape = [P, HEADS, 2, PAIRS, 2]
             nc.vector.tensor_tensor(
                 out=products[:, :, :, x].rearrange("p r h j s -> p h r j s"),
@@ -203,10 +215,6 @@ def tile_deepseekv4attention_pb_kernel(tc, hidden, wq, out):
                 .unsqueeze(1)
                 .to_broadcast(shape),
                 op=ALU.mult,
-            )
-            nc.scalar.copy(
-                out=result[:, :, x, :PLAIN],
-                in_=copied_acc[:].rearrange("p (h c) -> p h c", h=HEADS),
             )
 
         def add_tile(engine, heads, x, result, products):
@@ -249,12 +257,18 @@ def tile_deepseekv4attention_pb_kernel(tc, hidden, wq, out):
 
         earlier = None
         for n in range(GROUPS):
-            if n + AHEAD < GROUPS:
-                grouped = transpose_hidden(n + AHEAD)
+            if n == 0:
+                grouped = transpose_hidden(AHEAD)
             result = work.tile([P, HEADS, GROUP, HEAD_DIM], F32)
             products = work.tile([P, 2, HEADS, GROUP, PAIRS, 2], F32)
             by_tile = n >= GROUPS - 2
-            project(n, 0, result, products)
+            accs = [multiply_rotated(n, 0)]
+            if n > 0 and n + AHEAD < GROUPS:
+                grouped = transpose_hidden(n + AHEAD)
+            accs.append(multiply_rotated(n, 1))
+            for x in range(GROUP):
+                multiply_copied(n, x, result)
+            rotate(n, 0, accs[0], products)
             if n == GROUPS - 1:
                 add_tile(nc.vector, VECTOR_HEADS, 1, earlier[0], earlier[1])
                 nc.sync.dma_start(out=out_tiles[n * GROUP - 1], in_=earlier[0][:, :, 1, :])
@@ -264,7 +278,7 @@ def tile_deepseekv4attention_pb_kernel(tc, hidden, wq, out):
                     out=out_groups[n - 1], in_=earlier[0][:].rearrange("p h x d -> p h (x d)")
                 )
             add_tile(nc.gpsimd, GPSIMD_HEADS, 0, result, products)
-            project(n, 1, result, products)
+            rotate(n, 1, accs[1], products)
             if by_tile:
                 add_tile(nc.vector, VECTOR_HEADS, 0, result, products)
                 nc.sync.dma_start(out=out_tiles[n * GROUP], in_=result[:, :, 0, :])

@@ -244,14 +244,16 @@ def tile_deepseekv4attention_pb_kernel(tc, hidden, wq, out):
         copied_0 = regroup_copied(0, nc.scalar.copy)
         quantise_wq(0, ROTATED, rotated_0)
         rotated_1 = regroup_rotated(1)
-        quantise_wq(1, ROTATED, rotated_1)
         copied_1 = regroup_copied(1, nc.vector.tensor_copy)
         quantise_wq(0, COPIED, copied_0)
-        quantise_wq(1, COPIED, copied_1)
+        quantise_wq(1, ROTATED, rotated_1)
         quantised = {}
         for g in range(PASSES):
             keep_clock_up(w_raw[:, g, 0, :], 3)
-        for n in range(AHEAD):
+        grouped = transpose_hidden(0)
+        quantised[0] = quantise_hidden(grouped)
+        quantise_wq(1, COPIED, copied_1)
+        for n in range(1, AHEAD):
             quantised[n] = quantise_hidden(transpose_hidden(n))
         keep_clock_up(h_raw[AHEAD - 1][:], 2)
 

@@ -251,6 +251,7 @@ def tile_deepseekv4attention_pb_kernel(tc, hidden, wq, out):
         for g in range(PASSES):
             keep_clock_up(w_raw[:, g, 0, :], 3)
         grouped = transpose_hidden(0)
+        keep_clock_up(h_raw[0][:], 2)
         quantised[0] = quantise_hidden(grouped)
         quantise_wq(1, COPIED, copied_1)
         for n in range(1, AHEAD):

import math
from contextlib import ExitStack

import concourse.mybir as mybir
from concourse.masks import make_identity

F32 = mybir.dt.float32
BF16 = mybir.dt.bfloat16
I32 = mybir.dt.int32
U32 = mybir.dt.uint32
U8 = mybir.dt.uint8
FP8X4 = mybir.dt.float8_e4m3fn_x4
ALU = mybir.AluOpType
ACT = mybir.ActivationFunctionType

P = 128
TOKENS = 2048
HIDDEN = 1024
HEADS = 8
HEAD_DIM = 128
PAIRS = 32
PLAIN = HEAD_DIM - 2 * PAIRS
THETA = 10000.0

PACK = 4
HALVES = 2
K_PASS = P * PACK
PASSES = HIDDEN // K_PASS
BANK = 512

TILES = TOKENS // P
GROUP = 2
GROUPS = TILES // GROUP
GPSIMD_HEADS = slice(0, 6)
VECTOR_HEADS = slice(6, 8)
AHEAD = 2

ROTATED = 0
COPIED = 1

FLOPS = 2 * TOKENS * HIDDEN * HEADS * HEAD_DIM


def tile_deepseekv4attention_pb_kernel(tc, hidden, wq, out):
    nc = tc.nc
    with ExitStack() as ctx:
        keep = ctx.enter_context(tc.tile_pool(name="keep", bufs=1))
        w_stage = ctx.enter_context(tc.tile_pool(name="w_stage", bufs=2))
        h_stage = ctx.enter_context(tc.tile_pool(name="h_stage", bufs=AHEAD + 2))
        work = ctx.enter_context(tc.tile_pool(name="work", bufs=4))
        flipped_banks = ctx.enter_context(tc.psum_pool(name="flipped_banks", bufs=3))
        rotated_banks = ctx.enter_context(tc.psum_pool(name="rotated_banks", bufs=3))
        copied_banks = ctx.enter_context(tc.psum_pool(name="copied_banks", bufs=2))
        ctx.enter_context(tc.manual_schedule())

        hidden_groups = hidden[0].rearrange("(p n x) k -> n p (x k)", n=GROUPS, x=GROUP)
        out_groups = out[0].rearrange("h (p n x) d -> n p h (x d)", n=GROUPS, x=GROUP)
        out_tiles = out[0].rearrange("h (p i) d -> i p h d", i=TILES)

        h_raw = []
        for n in range(GROUPS):
            h_raw.append(keep.tile([P, GROUP * HIDDEN], BF16, name="h_raw%d" % n))
        w_raw = keep.tile([P, PASSES, PACK, HEADS * HEAD_DIM], BF16)

        def load_wq(g):
            nc.sync.dma_start(
                out=w_raw[:, g].rearrange("q t n -> q (t n)"),
                in_=wq[g * K_PASS : (g + 1) * K_PASS, :].rearrange("(q t) n -> q (t n)", q=P),
            )

        for g in range(PASSES):
            load_wq(g)
        for n in range(GROUPS):
            nc.sync.dma_start(out=h_raw[n][:], in_=hidden_groups[n])

        table = keep.tile([P, TILES, 2, 2, PAIRS], F32)

        warm = keep.tile([P, 1], F32)
        nc.vector.memset(warm[:], 0.0)
        nc.scalar.activation(out=warm[:], in_=warm[:], func=ACT.Sin)

        token_int = keep.tile([P, TILES], I32)
        nc.gpsimd.iota(token_int[:], pattern=[[1, TILES]], base=0, channel_multiplier=TILES)
        identity = keep.tile([P, P], F32)
        make_identity(nc, identity[:])
        token = keep.tile([P, TILES], F32)
        nc.vector.tensor_copy(out=token[:], in_=token_int[:])

        turns = keep.tile([P, TILES, PAIRS], F32)
        ratio = THETA ** (-1.0 / PAIRS)
        for j in range(4):
            nc.vector.tensor_scalar(
                out=turns[:, :, j], in0=token[:], scalar1=ratio**j / (2.0 * math.pi), scalar2=None,
                op0=ALU.mult,
            )
        for first in (4, 8, 12):
            nc.vector.tensor_scalar(
                out=turns[:, :, first : first + 4], in0=turns[:, :, 0:4], scalar1=ratio**first,
                scalar2=None, op0=ALU.mult,
            )
        nc.vector.tensor_scalar(
            out=turns[:, :, 16:32], in0=turns[:, :, 0:16], scalar1=ratio**16, scalar2=None,
            op0=ALU.mult,
        )
        whole = keep.tile([P, TILES, PAIRS], I32)
        nc.vector.tensor_copy(out=whole[:], in_=turns[:])
        fraction = keep.tile([P, TILES, PAIRS], F32)
        nc.vector.tensor_tensor(out=fraction[:], in0=turns[:], in1=whole[:], op=ALU.subtract)
        minus_abs = keep.tile([P, TILES, PAIRS], F32)
        nc.vector.scalar_tensor_tensor(
            out=minus_abs[:], in0=fraction[:], scalar=-1.0, in1=fraction[:], op0=ALU.mult, op1=ALU.min
        )
        turn = 2.0 * math.pi
        nc.scalar.activation(out=table[:, :, 0, 1, :], in_=fraction[:], func=ACT.Sin, scale=-turn)
        nc.scalar.activation(out=table[:, :, 1, 0, :], in_=fraction[:], func=ACT.Sin, scale=turn)
        for s in range(2):
            nc.scalar.activation(
                out=table[:, :, s, s, :], in_=minus_abs[:], func=ACT.Sin, scale=turn,
                bias=0.5 * math.pi,
            )

        def transpose_hidden(n):
            raw_words = h_raw[n][:].bitcast(F32).rearrange("m (x w) -> m x w", x=GROUP)
            grouped = h_stage.tile([P, GROUP * PASSES * P * PACK], BF16, align_bytes=64)
            grouped_words = grouped[:].bitcast(F32).rearrange(
                "q (x g m u) -> q x g m u", x=GROUP, g=PASSES, u=HALVES
            )
            for x in range(GROUP):
                flipped = flipped_banks.tile([P, PASSES * HALVES, P], F32)
                for g in range(PASSES):
                    for u in range(HALVES):
                        nc.tensor.transpose(
                            flipped[:, g * HALVES + u, :],
                            raw_words[:, x, g * HALVES * P + u : (g + 1) * HALVES * P : HALVES],
                            identity[:],
                        )
                nc.scalar.copy(
                    out=grouped_words[:, x],
                    in_=flipped[:].rearrange("q (g u) m -> q g m u", u=HALVES),
                )
            return grouped

        def quantise_hidden(grouped):
            codes = h_stage.tile([P, GROUP * PASSES * P], U32, align_bytes=64)
            scales = h_stage.tile([P, GROUP * PASSES * P], U8, align_bytes=64)
            nc.vector.quantize_mx(out=codes[:].bitcast(FP8X4), scales=scales[:], in_=grouped[:])
            return codes, scales

        w_codes = keep.tile([P, PASSES, 2, BANK], U32, align_bytes=64)
        w_scales = keep.tile([P, PASSES, 2, BANK], U8, align_bytes=64)

        def features_of_wq(g):
            return w_raw[:, g].rearrange("q t (h s c) -> q s h c t", h=HEADS, s=2)

        def regroup_rotated(g):
            grouped = w_stage.tile([P, BANK * PACK], BF16, align_bytes=64, tag="rotated")
            nc.vector.tensor_copy(
                out=grouped[:].rearrange("q (h r j t) -> q h r j t", r=2, h=HEADS, t=PACK),
                in_=features_of_wq(g)[:, 1].rearrange("q h (j r) t -> q h r j t", r=2),
            )
            return grouped

        def regroup_copied(g, copy):
            grouped = w_stage.tile([P, BANK * PACK], BF16, align_bytes=64, tag="copied")
            copy(
                out=grouped[:].rearrange("q (h c t) -> q h c t", h=HEADS, t=PACK),
                in_=features_of_wq(g)[:, 0],
            )
            return grouped

        def quantise_wq(g, part, grouped):
            nc.vector.quantize_mx(
                out=w_codes[:, g, part, :].bitcast(FP8X4),
                scales=w_scales[:, g, part, :],
                in_=grouped[:],
            )

        def multiply(n, x, part, acc):
            codes, scales = quantised[n]
            for g in range(PASSES):
                tokens = slice((x * PASSES + g) * P, (x * PASSES + g + 1) * P)
                nc.tensor.matmul_mx(
                    out=acc[:],
                    lhsT=codes[:, tokens].bitcast(FP8X4),
                    lhsT_scale=scales[:, tokens],
                    rhs=w_codes[:, g, part, :].bitcast(FP8X4),
                    rhs_scale=w_scales[:, g, part, :],
                    start=(g == 0),
                    stop=(g == PASSES - 1),
                )

        def multiply_rotated(n, x):
            rotated_acc = rotated_banks.tile([P, BANK], F32)
            multiply(n, x, ROTATED, rotated_acc)
            return rotated_acc

        def multiply_copied(n, x, result):
            copied_acc = copied_banks.tile([P, BANK], F32)
            multiply(n, x, COPIED, copied_acc)
            nc.scalar.copy(
                out=result[:, :, x, :PLAIN],
                in_=copied_acc[:].rearrange("p (h c) -> p h c", h=HEADS),
            )

        def rotate(n, x, rotated_acc, products):
            shape = [P, HEADS, 2, PAIRS, 2]
            nc.vector.tensor_tensor(
                out=products[:, :, :, x].rearrange("p r h j s -> p h r j s"),
                in0=rotated_acc[:]
                .rearrange("p (h r j) -> p h r j", r=2, h=HEADS)
                .unsqueeze(4)
                .to_broadcast(shape),
                in1=table[:, n * GROUP + x]
                .rearrange("p s r j -> p r j s")
                .unsqueeze(1)
                .to_broadcast(shape),
                op=ALU.mult,
            )

        def add_tile(engine, heads, x, result, products):
            engine.tensor_tensor(
                out=result[:, heads, x, PLAIN:],
                in0=products[:, 0, heads, x].rearrange("p h j s -> p h (j s)"),
                in1=products[:, 1, heads, x].rearrange("p h j s -> p h (j s)"),
                op=ALU.add,
            )

        def add_group(engine, heads, result, products):
            engine.tensor_tensor(
                out=result[:, heads, :, PLAIN:],
                in0=products[:, 0, heads].rearrange("p h x j s -> p h x (j s)"),
                in1=products[:, 1, heads].rearrange("p h x j s -> p h x (j s)"),
                op=ALU.add,
            )

        def keep_clock_up(fresh, count):
            unused = copied_banks.tile([P, BANK], F32, name="copied_acc")
            for c in range(count):
                nc.tensor.matmul(
                    unused[:], lhsT=fresh[:, :P], rhs=fresh[:, :BANK], start=True, stop=True
                )

        rotated_0 = regroup_rotated(0)
        copied_0 = regroup_copied(0, nc.scalar.copy)
        quantise_wq(0, ROTATED, rotated_0)
        rotated_1 = regroup_rotated(1)
        copied_1 = regroup_copied(1, nc.vector.tensor_copy)
        quantise_wq(0, COPIED, copied_0)
        quantise_wq(1, ROTATED, rotated_1)
        quantised = {}
        for g in range(PASSES):
            keep_clock_up(w_raw[:, g, 0, :], 3)
        grouped = transpose_hidden(0)
        keep_clock_up(h_raw[0][:], 2)
        quantised[0] = quantise_hidden(grouped)
        quantise_wq(1, COPIED, copied_1)
        for n in range(1, AHEAD):
            quantised[n] = quantise_hidden(transpose_hidden(n))
        keep_clock_up(h_raw[AHEAD - 1][:], 2)

        earlier = None
        for n in range(GROUPS):
            if n == 0:
                grouped = transpose_hidden(AHEAD)
            result = work.tile([P, HEADS, GROUP, HEAD_DIM], F32)
            products = work.tile([P, 2, HEADS, GROUP, PAIRS, 2], F32)
            by_tile = n >= GROUPS - 2
            accs = [multiply_rotated(n, 0)]
            if n > 0 and n + AHEAD < GROUPS:
                grouped = transpose_hidden(n + AHEAD)
            accs.append(multiply_rotated(n, 1))
            for x in range(GROUP):
                multiply_copied(n, x, result)
            rotate(n, 0, accs[0], products)
            if n == GROUPS - 1:
                add_tile(nc.vector, VECTOR_HEADS, 1, earlier[0], earlier[1])
                nc.sync.dma_start(out=out_tiles[n * GROUP - 1], in_=earlier[0][:, :, 1, :])
            elif n > 0:
                add_group(nc.vector, VECTOR_HEADS, earlier[0], earlier[1])
                nc.sync.dma_start(
                    out=out_groups[n - 1], in_=earlier[0][:].rearrange("p h x d -> p h (x d)")
                )
            add_tile(nc.gpsimd, GPSIMD_HEADS, 0, result, products)
            rotate(n, 1, accs[1], products)
            if by_tile:
                add_tile(nc.vector, VECTOR_HEADS, 0, result, products)
                nc.sync.dma_start(out=out_tiles[n * GROUP], in_=result[:, :, 0, :])
            else:
                quantised[n + AHEAD] = quantise_hidden(grouped)
            if n < GROUPS - 1:
                add_tile(nc.gpsimd, GPSIMD_HEADS, 1, result, products)
            earlier = (result, products)
        add_tile(nc.vector, slice(0, HEADS), 1, earlier[0], earlier[1])
        nc.sync.dma_start(out=out_tiles[TILES - 1], in_=earlier[0][:, :, 1, :])
